import numpy as np
import ml_dtypes


def mxq(x, axis, fmt="e4m3"):
    dtype, down = {"e4m3": (ml_dtypes.float8_e4m3fn, 7), "e5m2": (ml_dtypes.float8_e5m2, 14)}[fmt]
    v = np.moveaxis(np.asarray(x, np.float32).astype(ml_dtypes.bfloat16).astype(np.float64), axis, -1)
    blocks = v.reshape(v.shape[:-1] + (-1, 32))
    amax = np.abs(blocks).max(-1, keepdims=True)
    byte = np.maximum(np.where(amax > 0, np.frexp(amax)[1] - 1 + 127, 0) - down, 1)
    scale = np.exp2(byte - 127.0)
    codes = (blocks / scale).astype(np.float32).astype(dtype).astype(np.float64)
    return np.moveaxis((codes * scale).reshape(v.shape), -1, axis)


WIDE = False


def mx_kscale(k):
    if not WIDE:
        return np.ones(k)
    levels = np.array([10, -10, 5, -5, 0])
    a = np.random.permutation(np.resize(levels, k // 512 * 4)).reshape(k // 512, 4)
    idx = np.arange(k)
    return np.exp2(a[idx // 512, idx % 128 // 32])


BF16 = ml_dtypes.bfloat16


def bf(x):
    return np.asarray(x, np.float32).astype(BF16)


def f64(x):
    return np.asarray(x).astype(np.float64)


B, S, D, N, A, F = 32, 64, 512, 128, 128, 1024
LN_EPS = 1e-5


def setup_inputs():
    t = mx_kscale(F)
    return {
        "actions": bf(np.random.standard_normal((B, N, A))),
        "W_ae": bf(np.random.standard_normal((F, A)) / np.sqrt(A)),
        "b_ae": bf(np.random.standard_normal(F) * 0.4),
        "ln_g": bf((1.0 + 0.1 * np.random.standard_normal(F)) * t),
        "ln_b": bf(0.2 * np.random.standard_normal(F) * t),
        "Wv": bf(np.random.standard_normal((F, F)) / np.sqrt(F) / t[None, :]),
    }


def reference(actions, W_ae, b_ae, ln_g, ln_b, Wv):
    a = f64(actions) @ f64(W_ae).T + f64(b_ae)
    mu = a.mean(-1, keepdims=True)
    var = ((a - mu) ** 2).mean(-1, keepdims=True)
    a_n = (a - mu) / np.sqrt(var + LN_EPS) * f64(ln_g) + f64(ln_b)
    a_n = a_n
    return mxq(a_n, 2, "e4m3") @ mxq(f64(Wv), 1, "e4m3").T

@@ -1,0 +1,234 @@
+from contextlib import ExitStack
+
+import concourse.mybir as mybir
+from concourse.masks import make_identity
+
+F32 = mybir.dt.float32
+BF16 = mybir.dt.bfloat16
+U32 = mybir.dt.uint32
+U8 = mybir.dt.uint8
+FP8X4 = mybir.dt.float8_e4m3fn_x4
+ALU = mybir.AluOpType
+ACT = mybir.ActivationFunctionType
+AXIS = mybir.AxisListType
+
+P = 128
+TOKENS = 32 * 128
+A = 128
+F = 1024
+LN_EPS = 1e-5
+
+TILES = TOKENS // P
+GROUP = 4
+GROUPS = TILES // GROUP
+GROUP_TOKENS = GROUP * P
+CHUNKS = F // P
+PACK = 4
+PASSES = F // (P * PACK)
+BANK = 512
+HALVES = F // BANK
+
+FLOPS = 2 * TOKENS * A * F + 2 * TOKENS * F * F
+
+
+def tile_actionbindingattention_pa_t_kernel(tc, actions, W_ae, b_ae, ln_g, ln_b, Wv, out):
+    nc = tc.nc
+    x_dram = actions.rearrange("b n a -> (b n) a").rearrange("(p i) a -> p i a", i=TILES)
+    out_dram = out.rearrange("b n o -> (b n) o").rearrange("(p i) o -> p i o", i=TILES)
+
+    with ExitStack() as ctx:
+        const = ctx.enter_context(tc.tile_pool(name="const", bufs=1))
+        a_pool = ctx.enter_context(tc.tile_pool(name="a_pool", bufs=2 * GROUP))
+        n_pool = ctx.enter_context(tc.tile_pool(name="n_pool", bufs=2 * GROUP))
+        stat_pool = ctx.enter_context(tc.tile_pool(name="stat_pool", bufs=3))
+        work = ctx.enter_context(tc.tile_pool(name="work", bufs=2))
+        o_pool = ctx.enter_context(tc.tile_pool(name="o_pool", bufs=6))
+        psum_a = ctx.enter_context(tc.psum_pool(name="psum_a", bufs=3))
+        psum_t = ctx.enter_context(tc.psum_pool(name="psum_t", bufs=2))
+        psum_o = ctx.enter_context(tc.psum_pool(name="psum_o", bufs=3))
+
+        w_nat = const.tile([P, CHUNKS, A], BF16)
+        nc.sync.dma_start(out=w_nat[:], in_=W_ae.rearrange("(c p) a -> p c a", p=P))
+        x_nat = const.tile([P, TILES, A], BF16)
+        x_piece = TILES // 4
+        for q in range(4):
+            tiles_q = slice(q * x_piece, (q + 1) * x_piece)
+            nc.sync.dma_start(out=x_nat[:, tiles_q, :], in_=x_dram[:, tiles_q, :])
+        vec_rows = const.tile([P, P], BF16)
+        nc.vector.memset(vec_rows[:], 0.0)
+        nc.sync.dma_start(out=vec_rows[0:CHUNKS, :], in_=ln_g.rearrange("(c p) -> c p", p=P))
+        nc.sync.dma_start(out=vec_rows[CHUNKS : 2 * CHUNKS, :], in_=ln_b.rearrange("(c p) -> c p", p=P))
+        b_bc = const.tile([P, F], BF16)
+        nc.gpsimd.dma_start(out=b_bc[:], in_=b_ae.partition_broadcast(P))
+        wv_nat = const.tile([P, CHUNKS, F], BF16)
+        wv_dram = Wv.rearrange("(oc p) k -> p oc k", p=P)
+        for q in range(4):
+            nc.sync.dma_start(out=wv_nat[:, 2 * q : 2 * q + 2, :], in_=wv_dram[:, 2 * q : 2 * q + 2, :])
+
+        ident_bf = const.tile([P, P], BF16)
+        make_identity(nc, ident_bf[:])
+        ident_f32 = const.tile([P, P], F32)
+        make_identity(nc, ident_f32[:])
+        eps = const.tile([P, 1], F32)
+        nc.vector.memset(eps[:], LN_EPS)
+
+        wT_ps = psum_t.tile([P, CHUNKS, P], BF16, tag="t")
+        for c in range(CHUNKS):
+            nc.tensor.transpose(wT_ps[:, c, :], w_nat[:, c, :], ident_bf[:])
+        wT = const.tile([P, F], BF16)
+        nc.vector.tensor_copy(out=wT[:], in_=wT_ps[:].rearrange("p c f -> p (c f)"))
+
+        vec_ps = psum_t.tile([P, P], BF16, tag="t")
+        nc.tensor.transpose(vec_ps[:], vec_rows[:], ident_bf[:])
+        gain_shift = const.tile([P, 2 * CHUNKS], F32)
+        nc.vector.tensor_copy(out=gain_shift[:], in_=vec_ps[:, 0 : 2 * CHUNKS])
+
+        xT = const.tile([P, TILES, P], BF16)
+        for q in range(TILES // CHUNKS):
+            xT_ps = psum_a.tile([P, CHUNKS, P], BF16, tag="a")
+            for r in range(CHUNKS):
+                nc.tensor.transpose(xT_ps[:, r, :], x_nat[:, q * CHUNKS + r, :], ident_bf[:])
+            nc.scalar.copy(out=xT[:, q * CHUNKS : (q + 1) * CHUNKS, :], in_=xT_ps[:])
+
+        wv_grouped = const.tile([P, PASSES, F, PACK], BF16, align_bytes=64)
+        wv_codes = const.tile([P, PASSES, F], U32, align_bytes=64)
+        wv_scales = const.tile([P, PASSES, F], U8, align_bytes=64)
+        for oc in range(CHUNKS):
+            wvT_ps = psum_o.tile([P, CHUNKS, P], BF16, tag="o")
+            for kc in range(CHUNKS):
+                nc.tensor.transpose(wvT_ps[:, kc, :], wv_nat[:, oc, kc * P : (kc + 1) * P], ident_bf[:])
+            for g in range(PASSES):
+                copy = nc.vector.tensor_copy if g == 0 else nc.scalar.copy
+                copy(
+                    out=wv_grouped[:, g, oc * P : (oc + 1) * P, :],
+                    in_=wvT_ps[:, g * PACK : (g + 1) * PACK, :].rearrange("p j o -> p o j"),
+                )
+        for h in range(HALVES):
+            for g in range(PASSES):
+                cols = slice(h * BANK, (h + 1) * BANK)
+                nc.vector.quantize_mx(
+                    out=wv_codes[:, g, cols].bitcast(FP8X4),
+                    scales=wv_scales[:, g, cols],
+                    in_=wv_grouped[:, g, cols, :].rearrange("p o j -> p (o j)"),
+                )
+
+        def encode_and_normalise(group):
+            sums = stat_pool.tile([P, GROUP, HALVES], F32)
+            a_tiles = []
+            for r in range(GROUP):
+                a_sb = a_pool.tile([P, F], F32)
+                a_tiles.append(a_sb)
+                for h in range(HALVES):
+                    cols = slice(h * BANK, (h + 1) * BANK)
+                    a_ps = psum_a.tile([P, BANK], F32, tag="a")
+                    nc.tensor.matmul(
+                        out=a_ps[:], lhsT=xT[:, group * GROUP + r, :], rhs=wT[:, cols], start=True, stop=True
+                    )
+                    nc.vector.scalar_tensor_tensor(
+                        out=a_sb[:, cols],
+                        in0=a_ps[:],
+                        scalar=1.0,
+                        in1=b_bc[:, cols],
+                        op0=ALU.mult,
+                        op1=ALU.add,
+                        accum_out=sums[:, r, h : h + 1],
+                    )
+            total = stat_pool.tile([P, GROUP], F32)
+            nc.vector.tensor_reduce(out=total[:], in_=sums[:], axis=AXIS.X, op=ALU.add)
+            neg_mean = stat_pool.tile([P, GROUP], F32)
+            nc.vector.tensor_scalar(out=neg_mean[:], in0=total[:], scalar1=-1.0 / F, scalar2=None, op0=ALU.mult)
+            sum_sq = stat_pool.tile([P, GROUP], F32)
+            for r in range(GROUP):
+                squares = work.tile([P, F], BF16)
+                nc.scalar.activation(
+                    out=squares[:],
+                    in_=a_tiles[r][:],
+                    func=ACT.Square,
+                    bias=neg_mean[:, r : r + 1],
+                    scale=1.0,
+                    accum_out=sum_sq[:, r : r + 1],
+                )
+            std = stat_pool.tile([P, GROUP], F32)
+            nc.scalar.activation(out=std[:], in_=sum_sq[:], func=ACT.Sqrt, bias=eps[:], scale=1.0 / F)
+            rstd = stat_pool.tile([P, GROUP], F32)
+            nc.vector.reciprocal(out=rstd[:], in_=std[:])
+            shift = stat_pool.tile([P, GROUP], F32)
+            nc.vector.tensor_tensor(out=shift[:], in0=neg_mean[:], in1=rstd[:], op=ALU.mult)
+            n_tiles = []
+            for r in range(GROUP):
+                n_sb = n_pool.tile([P, F], F32)
+                n_tiles.append(n_sb)
+                nc.gpsimd.tensor_scalar(
+                    out=n_sb[:],
+                    in0=a_tiles[r][:],
+                    scalar1=rstd[:, r : r + 1],
+                    scalar2=shift[:, r : r + 1],
+                    op0=ALU.mult,
+                    op1=ALU.add,
+                )
+            return n_tiles
+
+        def transpose_and_quantise(n_tiles):
+            planes = work.tile([P, CHUNKS, GROUP_TOKENS], BF16)
+            for c in range(CHUNKS):
+                t_ps = psum_t.tile([P, GROUP_TOKENS], F32, tag="t")
+                for r in range(GROUP):
+                    nc.tensor.transpose(
+                        t_ps[:, r * P : (r + 1) * P], n_tiles[r][:, c * P : (c + 1) * P], ident_f32[:]
+                    )
+                nc.scalar.activation(
+                    out=planes[:, c, :],
+                    in_=t_ps[:],
+                    func=ACT.Identity,
+                    scale=gain_shift[:, c : c + 1],
+                    bias=gain_shift[:, CHUNKS + c : CHUNKS + c + 1],
+                )
+            grouped = work.tile([P, PASSES, GROUP_TOKENS, PACK], BF16, align_bytes=64)
+            codes = work.tile([P, PASSES, GROUP_TOKENS], U32, align_bytes=64)
+            scales = work.tile([P, PASSES, GROUP_TOKENS], U8, align_bytes=64)
+            for g in range(PASSES):
+                nc.vector.tensor_copy(
+                    out=grouped[:, g, :, :],
+                    in_=planes[:, g * PACK : (g + 1) * PACK, :].rearrange("p j w -> p w j"),
+                )
+            for g in range(PASSES):
+                nc.vector.quantize_mx(
+                    out=codes[:, g, :].bitcast(FP8X4),
+                    scales=scales[:, g, :],
+                    in_=grouped[:, g, :, :].rearrange("p w j -> p (w j)"),
+                )
+            return codes, scales
+
+        def project_and_store(group, codes, scales):
+            for r in range(GROUP):
+                tokens = slice(r * P, (r + 1) * P)
+                o_sb = o_pool.tile([P, F], F32)
+                for h in range(HALVES):
+                    cols = slice(h * BANK, (h + 1) * BANK)
+                    o_ps = psum_o.tile([P, BANK], F32, tag="o")
+                    for g in range(PASSES):
+                        nc.tensor.matmul_mx(
+                            out=o_ps[:],
+                            lhsT=codes[:, g, tokens].bitcast(FP8X4),
+                            lhsT_scale=scales[:, g, tokens],
+                            rhs=wv_codes[:, g, cols].bitcast(FP8X4),
+                            rhs_scale=wv_scales[:, g, cols],
+                            start=(g == 0),
+                            stop=(g == PASSES - 1),
+                        )
+                    if h == 0:
+                        nc.scalar.copy(out=o_sb[:, cols], in_=o_ps[:])
+                    else:
+                        nc.vector.tensor_copy(out=o_sb[:, cols], in_=o_ps[:])
+                nc.sync.dma_start(out=out_dram[:, group * GROUP + r, :], in_=o_sb[:])
+
+        normalised = {}
+        quantised = {}
+        for step in range(GROUPS + 2):
+            if step < GROUPS:
+                normalised[step] = encode_and_normalise(step)
+            if 1 <= step <= GROUPS:
+                quantised[step - 1] = transpose_and_quantise(normalised[step - 1])
+            if step >= 2:
+                codes, scales = quantised[step - 2]
+                project_and_store(step - 2, codes, scales)

@@ -27,6 +27,13 @@ PACK = 4
 PASSES = F // (P * PACK)
 BANK = 512
 HALVES = F // BANK
+X_PITCH = A + 32
+STAT_COLS = A + 2
+
+STATS_LEAD = 6
+TRANSPOSE_LAG = GROUP
+REGROUP_LAG = TRANSPOSE_LAG + 2
+PROJECT_LAG = TRANSPOSE_LAG + GROUP + 3
 
 FLOPS = 2 * TOKENS * A * F + 2 * TOKENS * F * F
 
@@ -38,28 +45,30 @@ def tile_actionbindingattention_pa_t_kernel(tc, actions, W_ae, b_ae, ln_g, ln_b,
 
     with ExitStack() as ctx:
         const = ctx.enter_context(tc.tile_pool(name="const", bufs=1))
-        a_pool = ctx.enter_context(tc.tile_pool(name="a_pool", bufs=2 * GROUP))
-        n_pool = ctx.enter_context(tc.tile_pool(name="n_pool", bufs=2 * GROUP))
         stat_pool = ctx.enter_context(tc.tile_pool(name="stat_pool", bufs=3))
+        bias_pool = ctx.enter_context(tc.tile_pool(name="bias_pool", bufs=6))
+        n_pool = ctx.enter_context(tc.tile_pool(name="n_pool", bufs=3 * GROUP))
         work = ctx.enter_context(tc.tile_pool(name="work", bufs=2))
-        o_pool = ctx.enter_context(tc.tile_pool(name="o_pool", bufs=6))
-        psum_a = ctx.enter_context(tc.psum_pool(name="psum_a", bufs=3))
+        o_pool = ctx.enter_context(tc.tile_pool(name="o_pool", bufs=4))
+        psum_y = ctx.enter_context(tc.psum_pool(name="psum_y", bufs=2))
+        psum_a = ctx.enter_context(tc.psum_pool(name="psum_a", bufs=2))
         psum_t = ctx.enter_context(tc.psum_pool(name="psum_t", bufs=2))
-        psum_o = ctx.enter_context(tc.psum_pool(name="psum_o", bufs=3))
+        psum_o = ctx.enter_context(tc.psum_pool(name="psum_o", bufs=2))
 
         w_nat = const.tile([P, CHUNKS, A], BF16)
         nc.sync.dma_start(out=w_nat[:], in_=W_ae.rearrange("(c p) a -> p c a", p=P))
-        x_nat = const.tile([P, TILES, A], BF16)
+        vec_rows = const.tile([P, P], BF16)
+        nc.vector.memset(vec_rows[:], 0.0)
+        for v, vec in enumerate((ln_g, ln_b, b_ae)):
+            nc.sync.dma_start(
+                out=vec_rows[v * CHUNKS : (v + 1) * CHUNKS, :], in_=vec.rearrange("(c p) -> c p", p=P)
+            )
+        x_aug = const.tile([P, TILES, X_PITCH], BF16)
+        nc.vector.memset(x_aug[:, :, A : A + 1], 2.0)
         x_piece = TILES // 4
         for q in range(4):
             tiles_q = slice(q * x_piece, (q + 1) * x_piece)
-            nc.sync.dma_start(out=x_nat[:, tiles_q, :], in_=x_dram[:, tiles_q, :])
-        vec_rows = const.tile([P, P], BF16)
-        nc.vector.memset(vec_rows[:], 0.0)
-        nc.sync.dma_start(out=vec_rows[0:CHUNKS, :], in_=ln_g.rearrange("(c p) -> c p", p=P))
-        nc.sync.dma_start(out=vec_rows[CHUNKS : 2 * CHUNKS, :], in_=ln_b.rearrange("(c p) -> c p", p=P))
-        b_bc = const.tile([P, F], BF16)
-        nc.gpsimd.dma_start(out=b_bc[:], in_=b_ae.partition_broadcast(P))
+            nc.sync.dma_start(out=x_aug[:, tiles_q, 0:A], in_=x_dram[:, tiles_q, :])
         wv_nat = const.tile([P, CHUNKS, F], BF16)
         wv_dram = Wv.rearrange("(oc p) k -> p oc k", p=P)
         for q in range(4):
@@ -69,166 +78,263 @@ def tile_actionbindingattention_pa_t_kernel(tc, actions, W_ae, b_ae, ln_g, ln_b,
         make_identity(nc, ident_bf[:])
         ident_f32 = const.tile([P, P], F32)
         make_identity(nc, ident_f32[:])
-        eps = const.tile([P, 1], F32)
-        nc.vector.memset(eps[:], LN_EPS)
+        b_bc = const.tile([P, F], BF16)
+        nc.gpsimd.dma_start(out=b_bc[:], in_=b_ae.partition_broadcast(P))
+        neg_mean_bf = const.tile([P, P], BF16)
+        nc.vector.memset(neg_mean_bf[:], -1.0 / F)
+        neg_mean_f32 = const.tile([P, P], F32)
+        nc.vector.memset(neg_mean_f32[:], -1.0 / F)
+
+        xT = const.tile([P, TILES, P], BF16)
+
+        def transpose_actions(q):
+            xT_ps = psum_a.tile([P, CHUNKS, P], BF16, tag="a")
+            for r in range(CHUNKS):
+                nc.tensor.transpose(xT_ps[:, r, :], x_aug[:, q * CHUNKS + r, 0:A], ident_bf[:])
+            nc.scalar.copy(out=xT[:, q * CHUNKS : (q + 1) * CHUNKS, :], in_=xT_ps[:])
 
         wT_ps = psum_t.tile([P, CHUNKS, P], BF16, tag="t")
         for c in range(CHUNKS):
             nc.tensor.transpose(wT_ps[:, c, :], w_nat[:, c, :], ident_bf[:])
         wT = const.tile([P, F], BF16)
-        nc.vector.tensor_copy(out=wT[:], in_=wT_ps[:].rearrange("p c f -> p (c f)"))
-
+        nc.scalar.copy(out=wT[:], in_=wT_ps[:].rearrange("p c f -> p (c f)"))
         vec_ps = psum_t.tile([P, P], BF16, tag="t")
         nc.tensor.transpose(vec_ps[:], vec_rows[:], ident_bf[:])
-        gain_shift = const.tile([P, 2 * CHUNKS], F32)
-        nc.vector.tensor_copy(out=gain_shift[:], in_=vec_ps[:, 0 : 2 * CHUNKS])
+        vec_cols = const.tile([P, 3 * CHUNKS], F32)
+        nc.vector.tensor_copy(out=vec_cols[:], in_=vec_ps[:, 0 : 3 * CHUNKS])
+        gain = vec_cols[:, 0:CHUNKS]
+        shift_f = vec_cols[:, CHUNKS : 2 * CHUNKS]
+        b_cols = vec_cols[:, 2 * CHUNKS : 3 * CHUNKS]
 
-        xT = const.tile([P, TILES, P], BF16)
-        for q in range(TILES // CHUNKS):
-            xT_ps = psum_a.tile([P, CHUNKS, P], BF16, tag="a")
-            for r in range(CHUNKS):
-                nc.tensor.transpose(xT_ps[:, r, :], x_nat[:, q * CHUNKS + r, :], ident_bf[:])
-            nc.scalar.copy(out=xT[:, q * CHUNKS : (q + 1) * CHUNKS, :], in_=xT_ps[:])
+        neg_wbar_ps = psum_y.tile([P, A], F32, tag="y")
+        for c in range(CHUNKS):
+            nc.tensor.matmul(
+                out=neg_wbar_ps[:], lhsT=neg_mean_bf[:], rhs=w_nat[:, c, :], start=(c == 0), stop=(c == CHUNKS - 1)
+            )
+        neg_b_ps = psum_y.tile([P, CHUNKS], F32, tag="y")
+        nc.tensor.matmul(out=neg_b_ps[:], lhsT=neg_mean_f32[:], rhs=b_cols, start=True, stop=True)
+        transpose_actions(0)
+        neg_bbar = const.tile([P, 1], F32)
+        nc.vector.tensor_reduce(out=neg_bbar[:], in_=neg_b_ps[:], axis=AXIS.X, op=ALU.add)
+        centred = const.tile([P, CHUNKS, A + 1], F32)
+        nc.vector.tensor_tensor(
+            out=centred[:, :, 0:A],
+            in0=w_nat[:],
+            in1=neg_wbar_ps[:].unsqueeze(1).to_broadcast([P, CHUNKS, A]),
+            op=ALU.add,
+        )
+        nc.vector.tensor_scalar(
+            out=centred[:, :, A], in0=b_cols, scalar1=neg_bbar[:], scalar2=None, op0=ALU.add
+        )
+        bc_sq = const.tile([P, CHUNKS], F32)
+        nc.vector.tensor_tensor(out=bc_sq[:], in0=centred[:, :, A], in1=centred[:, :, A], op=ALU.mult)
+        gram_ps = psum_y.tile([P, STAT_COLS], F32, tag="y")
+        for c in range(CHUNKS):
+            nc.tensor.matmul(
+                out=gram_ps[:, 0 : A + 1],
+                lhsT=centred[:, c, 0:A],
+                rhs=centred[:, c, :],
+                start=(c == 0),
+                stop=(c == CHUNKS - 1),
+            )
+        for c in range(CHUNKS):
+            nc.tensor.matmul(
+                out=gram_ps[:, A + 1 : A + 2],
+                lhsT=w_nat[:, c, :],
+                rhs=neg_mean_bf[:, 0:1],
+                start=(c == 0),
+                stop=(c == CHUNKS - 1),
+            )
+        neg_c0_ps = psum_y.tile([P, CHUNKS], F32, tag="y")
+        nc.tensor.matmul(out=neg_c0_ps[:], lhsT=neg_mean_f32[:], rhs=bc_sq[:], start=True, stop=True)
+        for q in range(1, TILES // CHUNKS):
+            transpose_actions(q)
+        stat_hi = const.tile([P, STAT_COLS], BF16)
+        nc.vector.tensor_copy(out=stat_hi[:], in_=gram_ps[:])
+        stat_lo = const.tile([P, STAT_COLS], BF16)
+        nc.vector.tensor_tensor(out=stat_lo[:], in0=gram_ps[:], in1=stat_hi[:], op=ALU.subtract)
+        neg_var_b = const.tile([P, 1], F32)
+        nc.vector.tensor_reduce(out=neg_var_b[:], in_=neg_c0_ps[:], axis=AXIS.X, op=ALU.add)
+        var_bias = const.tile([P, 1], F32)
+        nc.vector.tensor_scalar(
+            out=var_bias[:], in0=neg_var_b[:], scalar1=-1.0, scalar2=LN_EPS, op0=ALU.mult, op1=ALU.add
+        )
 
         wv_grouped = const.tile([P, PASSES, F, PACK], BF16, align_bytes=64)
         wv_codes = const.tile([P, PASSES, F], U32, align_bytes=64)
         wv_scales = const.tile([P, PASSES, F], U8, align_bytes=64)
-        for oc in range(CHUNKS):
+
+        def prepare_wv(oc):
             wvT_ps = psum_o.tile([P, CHUNKS, P], BF16, tag="o")
             for kc in range(CHUNKS):
                 nc.tensor.transpose(wvT_ps[:, kc, :], wv_nat[:, oc, kc * P : (kc + 1) * P], ident_bf[:])
             for g in range(PASSES):
-                copy = nc.vector.tensor_copy if g == 0 else nc.scalar.copy
-                copy(
+                copy_out = nc.vector.tensor_copy if g == 0 else nc.scalar.copy
+                copy_out(
                     out=wv_grouped[:, g, oc * P : (oc + 1) * P, :],
                     in_=wvT_ps[:, g * PACK : (g + 1) * PACK, :].rearrange("p j o -> p o j"),
                 )
-        for h in range(HALVES):
-            for g in range(PASSES):
-                cols = slice(h * BANK, (h + 1) * BANK)
-                nc.vector.quantize_mx(
-                    out=wv_codes[:, g, cols].bitcast(FP8X4),
-                    scales=wv_scales[:, g, cols],
-                    in_=wv_grouped[:, g, cols, :].rearrange("p o j -> p (o j)"),
+            if (oc + 1) * P % BANK == 0:
+                cols = slice((oc + 1) * P - BANK, (oc + 1) * P)
+                for g in range(PASSES):
+                    nc.vector.quantize_mx(
+                        out=wv_codes[:, g, cols].bitcast(FP8X4),
+                        scales=wv_scales[:, g, cols],
+                        in_=wv_grouped[:, g, cols, :].rearrange("p o j -> p (o j)"),
+                    )
+
+        stat_ps = {}
+        f_var = {}
+        rstd = {}
+        bias_rows = {}
+        n_tiles = {}
+        planes = {}
+        grouped = {}
+        quantised = {}
+
+        def statistics(pair):
+            group = pair * 2 // GROUP
+            if pair * 2 % GROUP == 0:
+                f_var_tile = stat_pool.tile([P, GROUP], F32)
+                f_var[group] = f_var_tile
+            y_ps = psum_y.tile([P, 2, STAT_COLS], F32, tag="y")
+            stat_ps[pair] = y_ps
+            for e in range(2):
+                nc.tensor.matmul(out=y_ps[:, e, :], lhsT=xT[:, 2 * pair + e, :], rhs=stat_hi[:], start=True, stop=False)
+                nc.tensor.matmul(out=y_ps[:, e, :], lhsT=xT[:, 2 * pair + e, :], rhs=stat_lo[:], start=False, stop=True)
+            for e in range(2):
+                tile_i = 2 * pair + e
+                products = work.tile([P, A + 1], F32)
+                nc.vector.scalar_tensor_tensor(
+                    out=products[:],
+                    in0=y_ps[:, e, 0 : A + 1],
+                    scalar=1.0,
+                    in1=x_aug[:, tile_i, 0 : A + 1],
+                    op0=ALU.mult,
+                    op1=ALU.mult,
+                    accum_out=f_var[group][:, tile_i % GROUP : tile_i % GROUP + 1],
                 )
 
-        def encode_and_normalise(group):
-            sums = stat_pool.tile([P, GROUP, HALVES], F32)
-            a_tiles = []
-            for r in range(GROUP):
-                a_sb = a_pool.tile([P, F], F32)
-                a_tiles.append(a_sb)
-                for h in range(HALVES):
-                    cols = slice(h * BANK, (h + 1) * BANK)
-                    a_ps = psum_a.tile([P, BANK], F32, tag="a")
-                    nc.tensor.matmul(
-                        out=a_ps[:], lhsT=xT[:, group * GROUP + r, :], rhs=wT[:, cols], start=True, stop=True
-                    )
-                    nc.vector.scalar_tensor_tensor(
-                        out=a_sb[:, cols],
-                        in0=a_ps[:],
-                        scalar=1.0,
-                        in1=b_bc[:, cols],
-                        op0=ALU.mult,
-                        op1=ALU.add,
-                        accum_out=sums[:, r, h : h + 1],
-                    )
-            total = stat_pool.tile([P, GROUP], F32)
-            nc.vector.tensor_reduce(out=total[:], in_=sums[:], axis=AXIS.X, op=ALU.add)
-            neg_mean = stat_pool.tile([P, GROUP], F32)
-            nc.vector.tensor_scalar(out=neg_mean[:], in0=total[:], scalar1=-1.0 / F, scalar2=None, op0=ALU.mult)
-            sum_sq = stat_pool.tile([P, GROUP], F32)
-            for r in range(GROUP):
-                squares = work.tile([P, F], BF16)
-                nc.scalar.activation(
-                    out=squares[:],
-                    in_=a_tiles[r][:],
-                    func=ACT.Square,
-                    bias=neg_mean[:, r : r + 1],
-                    scale=1.0,
-                    accum_out=sum_sq[:, r : r + 1],
-                )
+        def finish_statistics(group):
             std = stat_pool.tile([P, GROUP], F32)
-            nc.scalar.activation(out=std[:], in_=sum_sq[:], func=ACT.Sqrt, bias=eps[:], scale=1.0 / F)
-            rstd = stat_pool.tile([P, GROUP], F32)
-            nc.vector.reciprocal(out=rstd[:], in_=std[:])
-            shift = stat_pool.tile([P, GROUP], F32)
-            nc.vector.tensor_tensor(out=shift[:], in0=neg_mean[:], in1=rstd[:], op=ALU.mult)
-            n_tiles = []
+            nc.scalar.activation(out=std[:], in_=f_var[group][:], func=ACT.Sqrt, bias=var_bias[:], scale=1.0 / F)
+            rstd_tile = stat_pool.tile([P, GROUP], F32)
+            rstd[group] = rstd_tile
+            nc.vector.reciprocal(out=rstd_tile[:], in_=std[:])
+            shift_t = stat_pool.tile([P, GROUP], F32)
+            for e in range(GROUP // 2):
+                nc.vector.scalar_tensor_tensor(
+                    out=shift_t[:, 2 * e : 2 * e + 2],
+                    in0=stat_ps[group * GROUP // 2 + e][:, :, A + 1],
+                    scalar=neg_bbar[:],
+                    in1=rstd_tile[:, 2 * e : 2 * e + 2],
+                    op0=ALU.add,
+                    op1=ALU.mult,
+                )
             for r in range(GROUP):
-                n_sb = n_pool.tile([P, F], F32)
-                n_tiles.append(n_sb)
+                bias_tile = bias_pool.tile([P, F], F32)
+                bias_rows[group * GROUP + r] = bias_tile
                 nc.gpsimd.tensor_scalar(
-                    out=n_sb[:],
-                    in0=a_tiles[r][:],
-                    scalar1=rstd[:, r : r + 1],
-                    scalar2=shift[:, r : r + 1],
+                    out=bias_tile[:],
+                    in0=b_bc[:],
+                    scalar1=rstd_tile[:, r : r + 1],
+                    scalar2=shift_t[:, r : r + 1],
                     op0=ALU.mult,
                     op1=ALU.add,
                 )
-            return n_tiles
 
-        def transpose_and_quantise(n_tiles):
-            planes = work.tile([P, CHUNKS, GROUP_TOKENS], BF16)
-            for c in range(CHUNKS):
+        def encode(tile_i):
+            n_sb = n_pool.tile([P, F], F32)
+            n_tiles[tile_i] = n_sb
+            for h in range(HALVES):
+                cols = slice(h * BANK, (h + 1) * BANK)
+                a_ps = psum_a.tile([P, BANK], F32, tag="a")
+                nc.tensor.matmul(out=a_ps[:], lhsT=xT[:, tile_i, :], rhs=wT[:, cols], start=True, stop=True)
+                nc.vector.scalar_tensor_tensor(
+                    out=n_sb[:, cols],
+                    in0=a_ps[:],
+                    scalar=rstd[tile_i // GROUP][:, tile_i % GROUP : tile_i % GROUP + 1],
+                    in1=bias_rows[tile_i][:, cols],
+                    op0=ALU.mult,
+                    op1=ALU.add,
+                )
+
+        def transpose_chunks(group, first, count):
+            if first == 0:
+                planes_tile = work.tile([P, CHUNKS, GROUP_TOKENS], BF16)
+                planes[group] = planes_tile
+            for c in range(first, first + count):
                 t_ps = psum_t.tile([P, GROUP_TOKENS], F32, tag="t")
                 for r in range(GROUP):
                     nc.tensor.transpose(
-                        t_ps[:, r * P : (r + 1) * P], n_tiles[r][:, c * P : (c + 1) * P], ident_f32[:]
+                        t_ps[:, r * P : (r + 1) * P], n_tiles[group * GROUP + r][:, c * P : (c + 1) * P], ident_f32[:]
                     )
                 nc.scalar.activation(
-                    out=planes[:, c, :],
+                    out=planes[group][:, c, :],
                     in_=t_ps[:],
                     func=ACT.Identity,
-                    scale=gain_shift[:, c : c + 1],
-                    bias=gain_shift[:, CHUNKS + c : CHUNKS + c + 1],
+                    scale=gain[:, c : c + 1],
+                    bias=shift_f[:, c : c + 1],
                 )
-            grouped = work.tile([P, PASSES, GROUP_TOKENS, PACK], BF16, align_bytes=64)
-            codes = work.tile([P, PASSES, GROUP_TOKENS], U32, align_bytes=64)
-            scales = work.tile([P, PASSES, GROUP_TOKENS], U8, align_bytes=64)
-            for g in range(PASSES):
-                nc.vector.tensor_copy(
-                    out=grouped[:, g, :, :],
-                    in_=planes[:, g * PACK : (g + 1) * PACK, :].rearrange("p j w -> p w j"),
-                )
-            for g in range(PASSES):
-                nc.vector.quantize_mx(
-                    out=codes[:, g, :].bitcast(FP8X4),
-                    scales=scales[:, g, :],
-                    in_=grouped[:, g, :, :].rearrange("p w j -> p (w j)"),
-                )
-            return codes, scales
 
-        def project_and_store(group, codes, scales):
-            for r in range(GROUP):
-                tokens = slice(r * P, (r + 1) * P)
-                o_sb = o_pool.tile([P, F], F32)
-                for h in range(HALVES):
-                    cols = slice(h * BANK, (h + 1) * BANK)
-                    o_ps = psum_o.tile([P, BANK], F32, tag="o")
-                    for g in range(PASSES):
-                        nc.tensor.matmul_mx(
-                            out=o_ps[:],
-                            lhsT=codes[:, g, tokens].bitcast(FP8X4),
-                            lhsT_scale=scales[:, g, tokens],
-                            rhs=wv_codes[:, g, cols].bitcast(FP8X4),
-                            rhs_scale=wv_scales[:, g, cols],
-                            start=(g == 0),
-                            stop=(g == PASSES - 1),
-                        )
-                    if h == 0:
-                        nc.scalar.copy(out=o_sb[:, cols], in_=o_ps[:])
-                    else:
-                        nc.vector.tensor_copy(out=o_sb[:, cols], in_=o_ps[:])
-                nc.sync.dma_start(out=out_dram[:, group * GROUP + r, :], in_=o_sb[:])
+        def regroup(group, g):
+            grouped_tile = work.tile([P, GROUP_TOKENS, PACK], BF16, align_bytes=64, bufs=3)
+            grouped[(group, g)] = grouped_tile
+            nc.vector.tensor_copy(
+                out=grouped_tile[:].rearrange("p (c i) j -> p c j i", i=4),
+                in_=planes[group][:, g * PACK : (g + 1) * PACK, :].rearrange("p j (c i) -> p c j i", i=4),
+            )
 
-        normalised = {}
-        quantised = {}
-        for step in range(GROUPS + 2):
-            if step < GROUPS:
-                normalised[step] = encode_and_normalise(step)
-            if 1 <= step <= GROUPS:
-                quantised[step - 1] = transpose_and_quantise(normalised[step - 1])
-            if step >= 2:
-                codes, scales = quantised[step - 2]
-                project_and_store(step - 2, codes, scales)
+        def quantise(group, g):
+            if g == 0:
+                codes_tile = work.tile([P, PASSES, GROUP_TOKENS], U32, align_bytes=64)
+                scales_tile = work.tile([P, PASSES, GROUP_TOKENS], U8, align_bytes=64)
+                quantised[group] = (codes_tile, scales_tile)
+            codes, scales = quantised[group]
+            nc.vector.quantize_mx(
+                out=codes[:, g, :].bitcast(FP8X4),
+                scales=scales[:, g, :],
+                in_=grouped[(group, g)][:].rearrange("p w j -> p (w j)"),
+            )
+
+        def project(tile_i):
+            codes, scales = quantised[tile_i // GROUP]
+            tokens = slice(tile_i % GROUP * P, (tile_i % GROUP + 1) * P)
+            o_sb = o_pool.tile([P, F], F32)
+            for h in range(HALVES):
+                cols = slice(h * BANK, (h + 1) * BANK)
+                o_ps = psum_o.tile([P, BANK], F32, tag="o")
+                for g in range(PASSES):
+                    nc.tensor.matmul_mx(
+                        out=o_ps[:],
+                        lhsT=codes[:, g, tokens].bitcast(FP8X4),
+                        lhsT_scale=scales[:, g, tokens],
+                        rhs=wv_codes[:, g, cols].bitcast(FP8X4),
+                        rhs_scale=wv_scales[:, g, cols],
+                        start=(g == 0),
+                        stop=(g == PASSES - 1),
+                    )
+                nc.scalar.copy(out=o_sb[:, cols], in_=o_ps[:])
+            nc.sync.dma_start(out=out_dram[:, tile_i, :], in_=o_sb[:])
+
+        chunks_a_slot = CHUNKS // GROUP
+        for slot in range(-STATS_LEAD, TILES + PROJECT_LAG):
+            if 0 <= slot - PROJECT_LAG:
+                project(slot - PROJECT_LAG)
+            if 0 <= slot < TILES:
+                encode(slot)
+            ahead = slot + STATS_LEAD
+            if ahead < TILES and ahead % 2 == 0:
+                statistics(ahead // 2)
+            if ahead < TILES and ahead % GROUP == GROUP - 1:
+                finish_statistics(ahead // GROUP)
+            if ahead < CHUNKS:
+                prepare_wv(ahead)
+            behind = slot - TRANSPOSE_LAG
+            if 0 <= behind < TILES:
+                transpose_chunks(behind // GROUP, behind % GROUP * chunks_a_slot, chunks_a_slot)
+            behind = slot - REGROUP_LAG
+            if 0 <= behind < TILES and behind % 2 == 0:
+                regroup(behind // GROUP, behind % GROUP // 2)
+            if 0 <= behind < TILES and behind % 2 == 1:
+                quantise(behind // GROUP, behind % GROUP // 2)

@@ -44,6 +44,7 @@ def tile_actionbindingattention_pa_t_kernel(tc, actions, W_ae, b_ae, ln_g, ln_b,
     out_dram = out.rearrange("b n o -> (b n) o").rearrange("(p i) o -> p i o", i=TILES)
 
     with ExitStack() as ctx:
+        ctx.enter_context(tc.manual_schedule())
         const = ctx.enter_context(tc.tile_pool(name="const", bufs=1))
         stat_pool = ctx.enter_context(tc.tile_pool(name="stat_pool", bufs=3))
         bias_pool = ctx.enter_context(tc.tile_pool(name="bias_pool", bufs=6))

@@ -114,7 +114,8 @@ def tile_actionbindingattention_pa_t_kernel(tc, actions, W_ae, b_ae, ln_g, ln_b,
             )
         neg_b_ps = psum_y.tile([P, CHUNKS], F32, tag="y")
         nc.tensor.matmul(out=neg_b_ps[:], lhsT=neg_mean_f32[:], rhs=b_cols, start=True, stop=True)
-        transpose_actions(0)
+        for q in range(TILES // CHUNKS):
+            transpose_actions(q)
         neg_bbar = const.tile([P, 1], F32)
         nc.vector.tensor_reduce(out=neg_bbar[:], in_=neg_b_ps[:], axis=AXIS.X, op=ALU.add)
         centred = const.tile([P, CHUNKS, A + 1], F32)
@@ -148,8 +149,6 @@ def tile_actionbindingattention_pa_t_kernel(tc, actions, W_ae, b_ae, ln_g, ln_b,
             )
         neg_c0_ps = psum_y.tile([P, CHUNKS], F32, tag="y")
         nc.tensor.matmul(out=neg_c0_ps[:], lhsT=neg_mean_f32[:], rhs=bc_sq[:], start=True, stop=True)
-        for q in range(1, TILES // CHUNKS):
-            transpose_actions(q)
         stat_hi = const.tile([P, STAT_COLS], BF16)
         nc.vector.tensor_copy(out=stat_hi[:], in_=gram_ps[:])
         stat_lo = const.tile([P, STAT_COLS], BF16)
@@ -170,8 +169,7 @@ def tile_actionbindingattention_pa_t_kernel(tc, actions, W_ae, b_ae, ln_g, ln_b,
             for kc in range(CHUNKS):
                 nc.tensor.transpose(wvT_ps[:, kc, :], wv_nat[:, oc, kc * P : (kc + 1) * P], ident_bf[:])
             for g in range(PASSES):
-                copy_out = nc.vector.tensor_copy if g == 0 else nc.scalar.copy
-                copy_out(
+                nc.scalar.copy(
                     out=wv_grouped[:, g, oc * P : (oc + 1) * P, :],
                     in_=wvT_ps[:, g * PACK : (g + 1) * PACK, :].rearrange("p j o -> p o j"),
                 )
@@ -235,14 +233,16 @@ def tile_actionbindingattention_pa_t_kernel(tc, actions, W_ae, b_ae, ln_g, ln_b,
             for r in range(GROUP):
                 bias_tile = bias_pool.tile([P, F], F32)
                 bias_rows[group * GROUP + r] = bias_tile
-                nc.gpsimd.tensor_scalar(
-                    out=bias_tile[:],
-                    in0=b_bc[:],
-                    scalar1=rstd_tile[:, r : r + 1],
-                    scalar2=shift_t[:, r : r + 1],
-                    op0=ALU.mult,
-                    op1=ALU.add,
-                )
+                for h in range(HALVES):
+                    cols = slice(h * BANK, (h + 1) * BANK)
+                    nc.gpsimd.tensor_scalar(
+                        out=bias_tile[:, cols],
+                        in0=b_bc[:, cols],
+                        scalar1=rstd_tile[:, r : r + 1],
+                        scalar2=shift_t[:, r : r + 1],
+                        op0=ALU.mult,
+                        op1=ALU.add,
+                    )
 
         def encode(tile_i):
             n_sb = n_pool.tile([P, F], F32)
@@ -315,7 +315,10 @@ def tile_actionbindingattention_pa_t_kernel(tc, actions, W_ae, b_ae, ln_g, ln_b,
                         start=(g == 0),
                         stop=(g == PASSES - 1),
                     )
-                nc.scalar.copy(out=o_sb[:, cols], in_=o_ps[:])
+                if tile_i + PROJECT_LAG >= TILES and h == 1:
+                    nc.vector.tensor_copy(out=o_sb[:, cols], in_=o_ps[:])
+                else:
+                    nc.scalar.copy(out=o_sb[:, cols], in_=o_ps[:])
             nc.sync.dma_start(out=out_dram[:, tile_i, :], in_=o_sb[:])
 
         chunks_a_slot = CHUNKS // GROUP
@@ -329,8 +332,8 @@ def tile_actionbindingattention_pa_t_kernel(tc, actions, W_ae, b_ae, ln_g, ln_b,
                 statistics(ahead // 2)
             if ahead < TILES and ahead % GROUP == GROUP - 1:
                 finish_statistics(ahead // GROUP)
-            if ahead < CHUNKS:
-                prepare_wv(ahead)
+            if 0 <= slot < CHUNKS:
+                prepare_wv(slot)
             behind = slot - TRANSPOSE_LAG
             if 0 <= behind < TILES:
                 transpose_chunks(behind // GROUP, behind % GROUP * chunks_a_slot, chunks_a_slot)

@@ -315,7 +315,7 @@ def tile_actionbindingattention_pa_t_kernel(tc, actions, W_ae, b_ae, ln_g, ln_b,
                         start=(g == 0),
                         stop=(g == PASSES - 1),
                     )
-                if tile_i + PROJECT_LAG >= TILES and h == 1:
+                if h == 1 and (tile_i % 2 == 1 or tile_i + PROJECT_LAG >= TILES):
                     nc.vector.tensor_copy(out=o_sb[:, cols], in_=o_ps[:])
                 else:
                     nc.scalar.copy(out=o_sb[:, cols], in_=o_ps[:])

@@ -281,10 +281,12 @@ def tile_actionbindingattention_pa_t_kernel(tc, actions, W_ae, b_ae, ln_g, ln_b,
         def regroup(group, g):
             grouped_tile = work.tile([P, GROUP_TOKENS, PACK], BF16, align_bytes=64, bufs=3)
             grouped[(group, g)] = grouped_tile
-            nc.vector.tensor_copy(
-                out=grouped_tile[:].rearrange("p (c i) j -> p c j i", i=4),
-                in_=planes[group][:, g * PACK : (g + 1) * PACK, :].rearrange("p j (c i) -> p c j i", i=4),
-            )
+            split = GROUP_TOKENS - P
+            for copy_tokens, tokens in ((nc.vector.tensor_copy, slice(0, split)), (nc.scalar.copy, slice(split, GROUP_TOKENS))):
+                copy_tokens(
+                    out=grouped_tile[:, tokens, :].rearrange("p (c i) j -> p c j i", i=4),
+                    in_=planes[group][:, g * PACK : (g + 1) * PACK, tokens].rearrange("p j (c i) -> p c j i", i=4),
+                )
 
         def quantise(group, g):
             if g == 0:
@@ -315,7 +317,7 @@ def tile_actionbindingattention_pa_t_kernel(tc, actions, W_ae, b_ae, ln_g, ln_b,
                         start=(g == 0),
                         stop=(g == PASSES - 1),
                     )
-                if h == 1 and (tile_i % 2 == 1 or tile_i + PROJECT_LAG >= TILES):
+                if tile_i + PROJECT_LAG >= TILES and h == 1:
                     nc.vector.tensor_copy(out=o_sb[:, cols], in_=o_ps[:])
                 else:
                     nc.scalar.copy(out=o_sb[:, cols], in_=o_ps[:])

from contextlib import ExitStack

import concourse.mybir as mybir
from concourse.masks import make_identity

F32 = mybir.dt.float32
BF16 = mybir.dt.bfloat16
U32 = mybir.dt.uint32
U8 = mybir.dt.uint8
FP8X4 = mybir.dt.float8_e4m3fn_x4
ALU = mybir.AluOpType
ACT = mybir.ActivationFunctionType
AXIS = mybir.AxisListType

P = 128
TOKENS = 32 * 128
A = 128
F = 1024
LN_EPS = 1e-5

TILES = TOKENS // P
GROUP = 4
GROUPS = TILES // GROUP
GROUP_TOKENS = GROUP * P
CHUNKS = F // P
PACK = 4
PASSES = F // (P * PACK)
BANK = 512
HALVES = F // BANK
X_PITCH = A + 32
STAT_COLS = A + 2

STATS_LEAD = 6
TRANSPOSE_LAG = GROUP
REGROUP_LAG = TRANSPOSE_LAG + 2
PROJECT_LAG = TRANSPOSE_LAG + GROUP + 3

FLOPS = 2 * TOKENS * A * F + 2 * TOKENS * F * F


def tile_actionbindingattention_pa_t_kernel(tc, actions, W_ae, b_ae, ln_g, ln_b, Wv, out):
    nc = tc.nc
    x_dram = actions.rearrange("b n a -> (b n) a").rearrange("(p i) a -> p i a", i=TILES)
    out_dram = out.rearrange("b n o -> (b n) o").rearrange("(p i) o -> p i o", i=TILES)

    with ExitStack() as ctx:
        ctx.enter_context(tc.manual_schedule())
        const = ctx.enter_context(tc.tile_pool(name="const", bufs=1))
        stat_pool = ctx.enter_context(tc.tile_pool(name="stat_pool", bufs=3))
        bias_pool = ctx.enter_context(tc.tile_pool(name="bias_pool", bufs=6))
        n_pool = ctx.enter_context(tc.tile_pool(name="n_pool", bufs=3 * GROUP))
        work = ctx.enter_context(tc.tile_pool(name="work", bufs=2))
        o_pool = ctx.enter_context(tc.tile_pool(name="o_pool", bufs=4))
        psum_y = ctx.enter_context(tc.psum_pool(name="psum_y", bufs=2))
        psum_a = ctx.enter_context(tc.psum_pool(name="psum_a", bufs=2))
        psum_t = ctx.enter_context(tc.psum_pool(name="psum_t", bufs=2))
        psum_o = ctx.enter_context(tc.psum_pool(name="psum_o", bufs=2))

        w_nat = const.tile([P, CHUNKS, A], BF16)
        nc.sync.dma_start(out=w_nat[:], in_=W_ae.rearrange("(c p) a -> p c a", p=P))
        vec_rows = const.tile([P, P], BF16)
        nc.vector.memset(vec_rows[:], 0.0)
        for v, vec in enumerate((ln_g, ln_b, b_ae)):
            nc.sync.dma_start(
                out=vec_rows[v * CHUNKS : (v + 1) * CHUNKS, :], in_=vec.rearrange("(c p) -> c p", p=P)
            )
        x_aug = const.tile([P, TILES, X_PITCH], BF16)
        nc.vector.memset(x_aug[:, :, A : A + 1], 2.0)
        x_piece = TILES // 4
        for q in range(4):
            tiles_q = slice(q * x_piece, (q + 1) * x_piece)
            nc.sync.dma_start(out=x_aug[:, tiles_q, 0:A], in_=x_dram[:, tiles_q, :])
        wv_nat = const.tile([P, CHUNKS, F], BF16)
        wv_dram = Wv.rearrange("(oc p) k -> p oc k", p=P)
        for q in range(4):
            nc.sync.dma_start(out=wv_nat[:, 2 * q : 2 * q + 2, :], in_=wv_dram[:, 2 * q : 2 * q + 2, :])

        ident_bf = const.tile([P, P], BF16)
        make_identity(nc, ident_bf[:])
        ident_f32 = const.tile([P, P], F32)
        make_identity(nc, ident_f32[:])
        b_bc = const.tile([P, F], BF16)
        nc.gpsimd.dma_start(out=b_bc[:], in_=b_ae.partition_broadcast(P))
        neg_mean_bf = const.tile([P, P], BF16)
        nc.vector.memset(neg_mean_bf[:], -1.0 / F)
        neg_mean_f32 = const.tile([P, P], F32)
        nc.vector.memset(neg_mean_f32[:], -1.0 / F)

        xT = const.tile([P, TILES, P], BF16)

        def transpose_actions(q):
            xT_ps = psum_a.tile([P, CHUNKS, P], BF16, tag="a")
            for r in range(CHUNKS):
                nc.tensor.transpose(xT_ps[:, r, :], x_aug[:, q * CHUNKS + r, 0:A], ident_bf[:])
            nc.scalar.copy(out=xT[:, q * CHUNKS : (q + 1) * CHUNKS, :], in_=xT_ps[:])

        wT_ps = psum_t.tile([P, CHUNKS, P], BF16, tag="t")
        for c in range(CHUNKS):
            nc.tensor.transpose(wT_ps[:, c, :], w_nat[:, c, :], ident_bf[:])
        wT = const.tile([P, F], BF16)
        nc.scalar.copy(out=wT[:], in_=wT_ps[:].rearrange("p c f -> p (c f)"))
        vec_ps = psum_t.tile([P, P], BF16, tag="t")
        nc.tensor.transpose(vec_ps[:], vec_rows[:], ident_bf[:])
        vec_cols = const.tile([P, 3 * CHUNKS], F32)
        nc.vector.tensor_copy(out=vec_cols[:], in_=vec_ps[:, 0 : 3 * CHUNKS])
        gain = vec_cols[:, 0:CHUNKS]
        shift_f = vec_cols[:, CHUNKS : 2 * CHUNKS]
        b_cols = vec_cols[:, 2 * CHUNKS : 3 * CHUNKS]

        neg_wbar_ps = psum_y.tile([P, A], F32, tag="y")
        for c in range(CHUNKS):
            nc.tensor.matmul(
                out=neg_wbar_ps[:], lhsT=neg_mean_bf[:], rhs=w_nat[:, c, :], start=(c == 0), stop=(c == CHUNKS - 1)
            )
        neg_b_ps = psum_y.tile([P, CHUNKS], F32, tag="y")
        nc.tensor.matmul(out=neg_b_ps[:], lhsT=neg_mean_f32[:], rhs=b_cols, start=True, stop=True)
        for q in range(TILES // CHUNKS):
            transpose_actions(q)
        neg_bbar = const.tile([P, 1], F32)
        nc.vector.tensor_reduce(out=neg_bbar[:], in_=neg_b_ps[:], axis=AXIS.X, op=ALU.add)
        centred = const.tile([P, CHUNKS, A + 1], F32)
        nc.vector.tensor_tensor(
            out=centred[:, :, 0:A],
            in0=w_nat[:],
            in1=neg_wbar_ps[:].unsqueeze(1).to_broadcast([P, CHUNKS, A]),
            op=ALU.add,
        )
        nc.vector.tensor_scalar(
            out=centred[:, :, A], in0=b_cols, scalar1=neg_bbar[:], scalar2=None, op0=ALU.add
        )
        bc_sq = const.tile([P, CHUNKS], F32)
        nc.vector.tensor_tensor(out=bc_sq[:], in0=centred[:, :, A], in1=centred[:, :, A], op=ALU.mult)
        gram_ps = psum_y.tile([P, STAT_COLS], F32, tag="y")
        for c in range(CHUNKS):
            nc.tensor.matmul(
                out=gram_ps[:, 0 : A + 1],
                lhsT=centred[:, c, 0:A],
                rhs=centred[:, c, :],
                start=(c == 0),
                stop=(c == CHUNKS - 1),
            )
        for c in range(CHUNKS):
            nc.tensor.matmul(
                out=gram_ps[:, A + 1 : A + 2],
                lhsT=w_nat[:, c, :],
                rhs=neg_mean_bf[:, 0:1],
                start=(c == 0),
                stop=(c == CHUNKS - 1),
            )
        neg_c0_ps = psum_y.tile([P, CHUNKS], F32, tag="y")
        nc.tensor.matmul(out=neg_c0_ps[:], lhsT=neg_mean_f32[:], rhs=bc_sq[:], start=True, stop=True)
        stat_hi = const.tile([P, STAT_COLS], BF16)
        nc.vector.tensor_copy(out=stat_hi[:], in_=gram_ps[:])
        stat_lo = const.tile([P, STAT_COLS], BF16)
        nc.vector.tensor_tensor(out=stat_lo[:], in0=gram_ps[:], in1=stat_hi[:], op=ALU.subtract)
        neg_var_b = const.tile([P, 1], F32)
        nc.vector.tensor_reduce(out=neg_var_b[:], in_=neg_c0_ps[:], axis=AXIS.X, op=ALU.add)
        var_bias = const.tile([P, 1], F32)
        nc.vector.tensor_scalar(
            out=var_bias[:], in0=neg_var_b[:], scalar1=-1.0, scalar2=LN_EPS, op0=ALU.mult, op1=ALU.add
        )

        wv_grouped = const.tile([P, PASSES, F, PACK], BF16, align_bytes=64)
        wv_codes = const.tile([P, PASSES, F], U32, align_bytes=64)
        wv_scales = const.tile([P, PASSES, F], U8, align_bytes=64)

        def prepare_wv(oc):
            wvT_ps = psum_o.tile([P, CHUNKS, P], BF16, tag="o")
            for kc in range(CHUNKS):
                nc.tensor.transpose(wvT_ps[:, kc, :], wv_nat[:, oc, kc * P : (kc + 1) * P], ident_bf[:])
            for g in range(PASSES):
                nc.scalar.copy(
                    out=wv_grouped[:, g, oc * P : (oc + 1) * P, :],
                    in_=wvT_ps[:, g * PACK : (g + 1) * PACK, :].rearrange("p j o -> p o j"),
                )
            if (oc + 1) * P % BANK == 0:
                cols = slice((oc + 1) * P - BANK, (oc + 1) * P)
                for g in range(PASSES):
                    nc.vector.quantize_mx(
                        out=wv_codes[:, g, cols].bitcast(FP8X4),
                        scales=wv_scales[:, g, cols],
                        in_=wv_grouped[:, g, cols, :].rearrange("p o j -> p (o j)"),
                    )

        stat_ps = {}
        f_var = {}
        rstd = {}
        bias_rows = {}
        n_tiles = {}
        planes = {}
        grouped = {}
        quantised = {}

        def statistics(pair):
            group = pair * 2 // GROUP
            if pair * 2 % GROUP == 0:
                f_var_tile = stat_pool.tile([P, GROUP], F32)
                f_var[group] = f_var_tile
            y_ps = psum_y.tile([P, 2, STAT_COLS], F32, tag="y")
            stat_ps[pair] = y_ps
            for e in range(2):
                nc.tensor.matmul(out=y_ps[:, e, :], lhsT=xT[:, 2 * pair + e, :], rhs=stat_hi[:], start=True, stop=False)
                nc.tensor.matmul(out=y_ps[:, e, :], lhsT=xT[:, 2 * pair + e, :], rhs=stat_lo[:], start=False, stop=True)
            for e in range(2):
                tile_i = 2 * pair + e
                products = work.tile([P, A + 1], F32)
                nc.vector.scalar_tensor_tensor(
                    out=products[:],
                    in0=y_ps[:, e, 0 : A + 1],
                    scalar=1.0,
                    in1=x_aug[:, tile_i, 0 : A + 1],
                    op0=ALU.mult,
                    op1=ALU.mult,
                    accum_out=f_var[group][:, tile_i % GROUP : tile_i % GROUP + 1],
                )

        def finish_statistics(group):
            std = stat_pool.tile([P, GROUP], F32)
            nc.scalar.activation(out=std[:], in_=f_var[group][:], func=ACT.Sqrt, bias=var_bias[:], scale=1.0 / F)
            rstd_tile = stat_pool.tile([P, GROUP], F32)
            rstd[group] = rstd_tile
            nc.vector.reciprocal(out=rstd_tile[:], in_=std[:])
            shift_t = stat_pool.tile([P, GROUP], F32)
            for e in range(GROUP // 2):
                nc.vector.scalar_tensor_tensor(
                    out=shift_t[:, 2 * e : 2 * e + 2],
                    in0=stat_ps[group * GROUP // 2 + e][:, :, A + 1],
                    scalar=neg_bbar[:],
                    in1=rstd_tile[:, 2 * e : 2 * e + 2],
                    op0=ALU.add,
                    op1=ALU.mult,
                )
            for r in range(GROUP):
                bias_tile = bias_pool.tile([P, F], F32)
                bias_rows[group * GROUP + r] = bias_tile
                for h in range(HALVES):
                    cols = slice(h * BANK, (h + 1) * BANK)
                    nc.gpsimd.tensor_scalar(
                        out=bias_tile[:, cols],
                        in0=b_bc[:, cols],
                        scalar1=rstd_tile[:, r : r + 1],
                        scalar2=shift_t[:, r : r + 1],
                        op0=ALU.mult,
                        op1=ALU.add,
                    )

        def encode(tile_i):
            n_sb = n_pool.tile([P, F], F32)
            n_tiles[tile_i] = n_sb
            for h in range(HALVES):
                cols = slice(h * BANK, (h + 1) * BANK)
                a_ps = psum_a.tile([P, BANK], F32, tag="a")
                nc.tensor.matmul(out=a_ps[:], lhsT=xT[:, tile_i, :], rhs=wT[:, cols], start=True, stop=True)
                nc.vector.scalar_tensor_tensor(
                    out=n_sb[:, cols],
                    in0=a_ps[:],
                    scalar=rstd[tile_i // GROUP][:, tile_i % GROUP : tile_i % GROUP + 1],
                    in1=bias_rows[tile_i][:, cols],
                    op0=ALU.mult,
                    op1=ALU.add,
                )

        def transpose_chunks(group, first, count):
            if first == 0:
                planes_tile = work.tile([P, CHUNKS, GROUP_TOKENS], BF16)
                planes[group] = planes_tile
            for c in range(first, first + count):
                t_ps = psum_t.tile([P, GROUP_TOKENS], F32, tag="t")
                for r in range(GROUP):
                    nc.tensor.transpose(
                        t_ps[:, r * P : (r + 1) * P], n_tiles[group * GROUP + r][:, c * P : (c + 1) * P], ident_f32[:]
                    )
                nc.scalar.activation(
                    out=planes[group][:, c, :],
                    in_=t_ps[:],
                    func=ACT.Identity,
                    scale=gain[:, c : c + 1],
                    bias=shift_f[:, c : c + 1],
                )

        def regroup(group, g):
            grouped_tile = work.tile([P, GROUP_TOKENS, PACK], BF16, align_bytes=64, bufs=3)
            grouped[(group, g)] = grouped_tile
            split = GROUP_TOKENS - P
            for copy_tokens, tokens in ((nc.vector.tensor_copy, slice(0, split)), (nc.scalar.copy, slice(split, GROUP_TOKENS))):
                copy_tokens(
                    out=grouped_tile[:, tokens, :].rearrange("p (c i) j -> p c j i", i=4),
                    in_=planes[group][:, g * PACK : (g + 1) * PACK, tokens].rearrange("p j (c i) -> p c j i", i=4),
                )

        def quantise(group, g):
            if g == 0:
                codes_tile = work.tile([P, PASSES, GROUP_TOKENS], U32, align_bytes=64)
                scales_tile = work.tile([P, PASSES, GROUP_TOKENS], U8, align_bytes=64)
                quantised[group] = (codes_tile, scales_tile)
            codes, scales = quantised[group]
            nc.vector.quantize_mx(
                out=codes[:, g, :].bitcast(FP8X4),
                scales=scales[:, g, :],
                in_=grouped[(group, g)][:].rearrange("p w j -> p (w j)"),
            )

        def project(tile_i):
            codes, scales = quantised[tile_i // GROUP]
            tokens = slice(tile_i % GROUP * P, (tile_i % GROUP + 1) * P)
            o_sb = o_pool.tile([P, F], F32)
            for h in range(HALVES):
                cols = slice(h * BANK, (h + 1) * BANK)
                o_ps = psum_o.tile([P, BANK], F32, tag="o")
                for g in range(PASSES):
                    nc.tensor.matmul_mx(
                        out=o_ps[:],
                        lhsT=codes[:, g, tokens].bitcast(FP8X4),
                        lhsT_scale=scales[:, g, tokens],
                        rhs=wv_codes[:, g, cols].bitcast(FP8X4),
                        rhs_scale=wv_scales[:, g, cols],
                        start=(g == 0),
                        stop=(g == PASSES - 1),
                    )
                if tile_i + PROJECT_LAG >= TILES and h == 1:
                    nc.vector.tensor_copy(out=o_sb[:, cols], in_=o_ps[:])
                else:
                    nc.scalar.copy(out=o_sb[:, cols], in_=o_ps[:])
            nc.sync.dma_start(out=out_dram[:, tile_i, :], in_=o_sb[:])

        chunks_a_slot = CHUNKS // GROUP
        for slot in range(-STATS_LEAD, TILES + PROJECT_LAG):
            if 0 <= slot - PROJECT_LAG:
                project(slot - PROJECT_LAG)
            if 0 <= slot < TILES:
                encode(slot)
            ahead = slot + STATS_LEAD
            if ahead < TILES and ahead % 2 == 0:
                statistics(ahead // 2)
            if ahead < TILES and ahead % GROUP == GROUP - 1:
                finish_statistics(ahead // GROUP)
            if 0 <= slot < CHUNKS:
                prepare_wv(slot)
            behind = slot - TRANSPOSE_LAG
            if 0 <= behind < TILES:
                transpose_chunks(behind // GROUP, behind % GROUP * chunks_a_slot, chunks_a_slot)
            behind = slot - REGROUP_LAG
            if 0 <= behind < TILES and behind % 2 == 0:
                regroup(behind // GROUP, behind % GROUP // 2)
            if 0 <= behind < TILES and behind % 2 == 1:
                quantise(behind // GROUP, behind % GROUP // 2)
